import numpy as np
import ml_dtypes


def mxq(x, axis, fmt="e4m3"):
    dtype, down = {"e4m3": (ml_dtypes.float8_e4m3fn, 7), "e5m2": (ml_dtypes.float8_e5m2, 14)}[fmt]
    v = np.moveaxis(np.asarray(x, np.float32).astype(ml_dtypes.bfloat16).astype(np.float64), axis, -1)
    blocks = v.reshape(v.shape[:-1] + (-1, 32))
    amax = np.abs(blocks).max(-1, keepdims=True)
    byte = np.maximum(np.where(amax > 0, np.frexp(amax)[1] - 1 + 127, 0) - down, 1)
    scale = np.exp2(byte - 127.0)
    codes = (blocks / scale).astype(np.float32).astype(dtype).astype(np.float64)
    return np.moveaxis((codes * scale).reshape(v.shape), -1, axis)


WIDE = False


def mx_kscale(k):
    if not WIDE:
        return np.ones(k)
    levels = np.array([10, -10, 5, -5, 0])
    if k % 512:
        return np.exp2(np.random.permutation(np.resize(levels, k // 32))).repeat(32)
    a = np.empty((k // 512, 16))
    for p in range(k // 512):
        a[p, :8] = np.random.permutation(np.resize(levels, 8))
        for g in range(8):
            far = levels[np.abs(levels - a[p, g]) >= 10]
            a[p, g + 8] = far[np.random.randint(len(far))]
    return np.exp2(a.ravel()).repeat(32)


BF16 = ml_dtypes.bfloat16


def bf(x):
    return np.asarray(x, np.float32).astype(BF16)


def f64(x):
    return np.asarray(x).astype(np.float64)


B, IN, H, NS, SS, CS, NA = 1024, 256, 2048, 4, 8, 128, 3
NC = NS * CS


def setup_inputs():
    s = mx_kscale(H)
    return {
        "h": bf(np.tanh(np.random.standard_normal((B, H))) * s),
        "act_logits": bf(np.random.standard_normal((B, NS * NA)) * 1.5),
        "stacks": bf(np.random.standard_normal((B, NS, SS, CS)) * 1.5),
        "W_push": bf(np.random.standard_normal((NC, H)) * 5.0 / np.sqrt(H) / s),
        "b_push": bf(np.random.standard_normal(NC) * 0.7),
    }


def core(h, act_logits, stacks, W_push, b_push):
    st = f64(stacks)
    push = ((mxq(f64(h), 1, "e4m3") @ mxq(f64(W_push), 1, "e4m3").T) + f64(b_push)).reshape(B, NS, CS)
    lg = f64(act_logits)
    e = np.exp(lg - lg.max(-1, keepdims=True))
    act = (e / e.sum(-1, keepdims=True)).reshape(B, NS, NA)
    pa, po, no = act[..., 0][..., None], act[..., 1][..., None], act[..., 2][..., None]
    top_new = pa * push + po * st[:, :, 1, :] + no * st[:, :, 0, :]
    zeros_tail = np.zeros((B, NS, 1, CS))
    pop_rest = np.concatenate([st[:, :, 2:, :], zeros_tail], axis=2)
    rest = (pa[:, :, :, None] * st[:, :, :-1, :]
            + po[:, :, :, None] * pop_rest
            + no[:, :, :, None] * st[:, :, 1:, :])
    return np.concatenate([top_new[:, :, None, :], rest], axis=2)


def e4m3fn_bytes(y):
    return np.clip(np.asarray(y, np.float64), -448.0, 448.0).astype(np.float32).astype(ml_dtypes.float8_e4m3fn).view(np.uint8)


def reference(h, act_logits, stacks, W_push, b_push):
    out = core(h, act_logits, stacks, W_push, b_push)
    s = np.max(np.abs(out), axis=-1, keepdims=True) / 448.0
    return out, e4m3fn_bytes(out / s)

@@ -1,0 +1,412 @@
+from contextlib import ExitStack
+
+import concourse.mybir as mybir
+from concourse.masks import make_identity
+
+B, H, NS, SS, CS, NA = 1024, 2048, 4, 8, 128, 3
+NC = NS * CS
+P = 128
+NT = B // P
+PACK = 4
+K_PASS = P * PACK
+NPASS = H // K_PASS
+UNIT = SS * CS
+NU = NT * NS
+NH = NT * 2
+L = NS * NA
+HR = 2 * SS
+OUT_BUFS = 8
+CV_STEADY = 0
+CV_TAIL = {13: 0, 14: 8}
+CV_LAST = 12
+
+FLOPS = 2 * B * H * NC + 5 * B * NS * SS * CS
+
+F32 = mybir.dt.float32
+BF16 = mybir.dt.bfloat16
+U32 = mybir.dt.uint32
+U8 = mybir.dt.uint8
+FP8X4 = mybir.dt.float8_e4m3fn_x4
+FP8 = mybir.dt.float8_e4m3fn
+ALU = mybir.AluOpType
+ACT = mybir.ActivationFunctionType
+AX = mybir.AxisListType
+ENG = mybir.EngineType
+
+
+def tile_stackrnncore_pa_kernel(tc, h, act_logits, stacks, W_push, b_push, out_0, out_1):
+    nc = tc.nc
+    h_v = h.rearrange("(p t) k -> p t k", t=NT)
+    lg_v = act_logits.rearrange("(p t) l -> p (t l)", t=NT)
+    st_v = stacks.rearrange("(p t) n i c -> p t n (i c)", t=NT)
+    w_v = W_push.rearrange("(j r) k -> r j k", r=P)
+    o0_v = out_0.rearrange("(p t) (a b) i c -> p (t a) (b i c)", t=NT, a=2)
+    o1_v = out_1.rearrange("(p t) (a b) i c -> p (t a) (b i c)", t=NT, a=2)
+
+    with ExitStack() as ctx:
+        const = ctx.enter_context(tc.tile_pool(name="const", bufs=1))
+        hgp = ctx.enter_context(tc.tile_pool(name="hgp", bufs=2))
+        hcp = ctx.enter_context(tc.tile_pool(name="hcp", bufs=3))
+        pbp = ctx.enter_context(tc.tile_pool(name="pbp", bufs=3))
+        outp = ctx.enter_context(tc.tile_pool(name="outp", bufs=OUT_BUFS))
+        stat = ctx.enter_context(tc.tile_pool(name="stat", bufs=6))
+        xtp = ctx.enter_context(tc.psum_pool(name="xtp", bufs=4))
+        accp = ctx.enter_context(tc.psum_pool(name="accp", bufs=2))
+        bpp = ctx.enter_context(tc.psum_pool(name="bpp", bufs=1))
+
+        st = {}
+        hraw = []
+        hgs = {}
+        hq = {}
+        accs = {}
+        pbs = {}
+        os_ = {}
+        qts = {}
+        stats = {}
+        qs = {}
+        late = {}
+
+        lg = const.tile([P, NT * L], BF16, name="lg")
+        zero = const.tile([P, 1], F32, name="zero")
+        warm = const.tile([P, 1], F32, name="warm")
+        ident = const.tile([P, P], F32, name="ident")
+        ones = const.tile([P, P], BF16, name="ones")
+        brow = const.tile([P, NC], BF16, name="brow")
+        bias = const.tile([P, NC], F32, name="bias")
+        act = const.tile([P, NT, L], F32, name="act")
+        wc = const.tile([P, NPASS * NC], U32, name="wc", align_bytes=64)
+        ws = const.tile([P, NPASS * NC], U8, name="ws", align_bytes=64)
+
+        def wgt(k, a):
+            t, n = divmod(k, NS)
+            return act[:, t, NA * n + a : NA * n + a + 1]
+
+        def uo(k):
+            return os_[k // 2][:, k % 2, :, :]
+
+        def h_trans(t):
+            hg = hgp.tile([P, NPASS * P * PACK], BF16, name="hg", align_bytes=64)
+            hgw = hg[:].bitcast(F32).rearrange("p (g r u) -> p g r u", g=NPASS, u=2)
+            words = hraw[t][:].bitcast(F32)
+            for gg in (0, 2):
+                xt = xtp.tile([P, 2, 2, P], F32, name="xt")
+                for a in range(2):
+                    g = gg + a
+                    for u in range(2):
+                        nc.tensor.transpose(out=xt[:, a, u, :], in_=words[:, 256 * g + u : 256 * (g + 1) : 2], identity=ident[:])
+                nc.scalar.copy(out=hgw[:, gg : gg + 2, :, :], in_=xt[:].rearrange("p a u r -> p a r u"))
+            hgs[t] = hg
+
+        def h_quant(t):
+            hc = hcp.tile([P, NPASS * P], U32, name="hc", align_bytes=64)
+            hs = hcp.tile([P, NPASS * P], U8, name="hs", align_bytes=64)
+            nc.vector.quantize_mx(out=hc[:].bitcast(FP8X4), scales=hs[:], in_=hgs[t][:])
+            hq[t] = (hc, hs)
+
+        def mm(t):
+            hc, hs = hq[t]
+            acc = accp.tile([P, NC], F32, name="acc")
+            for g in range(NPASS):
+                nc.tensor.matmul_mx(
+                    out=acc[:],
+                    lhsT=hc[:, g * P : (g + 1) * P].bitcast(FP8X4),
+                    lhsT_scale=hs[:, g * P : (g + 1) * P],
+                    rhs=wc[:, g * NC : (g + 1) * NC].bitcast(FP8X4),
+                    rhs_scale=ws[:, g * NC : (g + 1) * NC],
+                    start=(g == 0),
+                    stop=(g == NPASS - 1),
+                )
+            accs[t] = acc
+
+        def badd(t):
+            pb = pbp.tile([P, NC], F32, name="pb")
+            nc.vector.tensor_tensor(out=pb[:], in0=accs[t][:], in1=bias[:], op=ALU.add)
+            pbs[t] = pb
+
+        def prod_rest(k, lo=1, hi=SS):
+            if k // 2 not in os_:
+                o = outp.tile([P, 2, SS, CS], F32, name="o")
+                os_[k // 2] = o
+            sv = st[divmod(k, NS)]
+            nc.scalar.activation(out=uo(k)[:, lo:hi, :], in_=sv[:, lo - 1 : hi - 1, :], func=ACT.Copy, scale=wgt(k, 0))
+
+        def vprod_rest(k):
+            if k // 2 not in os_:
+                o = outp.tile([P, 2, SS, CS], F32, name="o")
+                os_[k // 2] = o
+            sv = st[divmod(k, NS)]
+            nc.vector.tensor_scalar(out=uo(k)[:, 1:SS, :], in0=sv[:, 0 : SS - 1, :], scalar1=wgt(k, 0), scalar2=None, op0=ALU.mult)
+
+        def prod_top(k):
+            t, n = divmod(k, NS)
+            nc.scalar.activation(out=uo(k)[:, 0, :], in_=pbs[t][:, n * CS : (n + 1) * CS], func=ACT.Copy, scale=wgt(k, 0))
+
+        def qprod(k, lo):
+            if k // 2 not in qts:
+                qt = late["qtp"].tile([P, 2, SS - 1, CS], F32, name="qt")
+                qts[k // 2] = qt
+            sv = st[divmod(k, NS)]
+            nc.scalar.activation(out=qts[k // 2][:, k % 2, lo : SS - 1, :], in_=sv[:, lo + 1 : SS, :], func=ACT.Copy, scale=wgt(k, 1))
+
+        def gadd(k, lo):
+            o = uo(k)
+            nc.gpsimd.tensor_tensor(out=o[:, lo : SS - 1, :], in0=o[:, lo : SS - 1, :], in1=qts[k // 2][:, k % 2, lo : SS - 1, :], op=ALU.add)
+
+        def t1(k, lo, hi):
+            o = uo(k)
+            sv = st[divmod(k, NS)]
+            nc.vector.scalar_tensor_tensor(out=o[:, lo:hi, :], in0=sv[:, lo:hi, :], scalar=wgt(k, 2), in1=o[:, lo:hi, :], op0=ALU.mult, op1=ALU.add)
+
+        def t2(k, lo, hi):
+            o = uo(k)
+            sv = st[divmod(k, NS)]
+            nc.vector.scalar_tensor_tensor(out=o[:, lo:hi, :], in0=sv[:, lo + 1 : hi + 1, :], scalar=wgt(k, 1), in1=o[:, lo:hi, :], op0=ALU.mult, op1=ALU.add)
+
+        def store0(m):
+            nc.sync.dma_start(out=o0_v[:, m, :], in_=os_[m][:].rearrange("p b i c -> p (b i c)"))
+
+        def red(m, b0=0, b1=2):
+            if b0 == 0:
+                am = stat.tile([P, HR], F32, name="am")
+                rc = stat.tile([P, HR], F32, name="rc")
+                r4 = stat.tile([P, HR], F32, name="r4")
+                stats[m] = (am, rc, r4)
+            am = stats[m][0]
+            nc.vector.tensor_reduce(out=am[:, b0 * SS : b1 * SS], in_=os_[m][:, b0:b1, :, :].rearrange("p b i c -> p (b i) c"), axis=AX.X, op=ALU.max, apply_absolute_value=True)
+
+        def rcp(m):
+            am, rc, r4 = stats[m]
+            nc.vector.reciprocal(out=rc[:], in_=am[:])
+
+        def mul(m):
+            am, rc, r4 = stats[m]
+            nc.scalar.activation(out=r4[:], in_=rc[:], func=ACT.Copy, scale=448.0)
+            q = late["qp"].tile([P, HR, CS], FP8, name="q")
+            qs[m] = q
+
+        def vmul(m):
+            am, rc, r4 = stats[m]
+            nc.vector.tensor_scalar(out=r4[:], in0=rc[:], scalar1=448.0, scalar2=None, op0=ALU.mult)
+            q = late["qp"].tile([P, HR, CS], FP8, name="q")
+            qs[m] = q
+
+        def scasts(m, cv):
+            r4 = stats[m][2]
+            ov = os_[m][:].rearrange("p b i c -> p (b i) c")
+            for j in range(cv, HR):
+                nc.scalar.activation(out=qs[m][:, j, :], in_=ov[:, j, :], func=ACT.Identity, scale=r4[:, j : j + 1], bias=zero[:, 0:1], saturate=False)
+
+        def vcasts(m, cv, c0=0):
+            r4 = stats[m][2]
+            ov = os_[m][:].rearrange("p b i c -> p (b i) c")
+            for j in range(c0, cv):
+                nc.vector.tensor_scalar(out=qs[m][:, j, :], in0=ov[:, j, :], scalar1=r4[:, j : j + 1], scalar2=None, op0=ALU.mult, saturate=False)
+
+        def store1(m, j0=0, j1=HR):
+            nc.sync.dma_start(out=o1_v[:, m, j0 * CS : j1 * CS], in_=qs[m][:, j0:j1, :].bitcast(U8).rearrange("p j c -> p (j c)"))
+
+        def tops(ks):
+            for k in ks:
+                prod_top(k)
+            for k in ks:
+                t1(k, 0, 1)
+            for k in ks:
+                t2(k, 0, 1)
+
+        nc.sync.dma_start(out=lg[:], in_=lg_v)
+        for n in range(NS):
+            s0 = const.tile([P, UNIT], BF16, name="st0_%d" % n)
+            nc.sync.dma_start(out=s0[:], in_=st_v[:, 0, n, :])
+            st[(0, n)] = s0[:].rearrange("p (i c) -> p i c", c=CS)
+        nc.gpsimd.memset(brow[:], 0.0)
+        nc.sync.dma_start(out=brow[0:1, :], in_=b_push.rearrange("(o n) -> o n", o=1))
+
+        with tc.tile_pool(name="wtmp", bufs=1) as wtmp:
+            wraw = []
+            for j in range(NS):
+                wr = wtmp.tile([P, H], BF16, name="wraw%d" % j)
+                nc.sync.dma_start(out=wr[:], in_=w_v[:, j, :])
+                wraw.append(wr)
+            for t in range(NT):
+                hr = const.tile([P, H], BF16, name="hraw%d" % t)
+                nc.sync.dma_start(out=hr[:], in_=h_v[:, t, :])
+                hraw.append(hr)
+                if t + 1 < NT:
+                    s1 = const.tile([P, NS, UNIT], BF16, name="st%d" % (t + 1))
+                    nc.sync.dma_start(out=s1[:], in_=st_v[:, t + 1, :, :])
+                    for n in range(NS):
+                        st[(t + 1, n)] = s1[:, n, :].rearrange("p (i c) -> p i c", c=CS)
+
+            nc.vector.memset(zero[:], 0.0)
+            nc.scalar.activation(out=warm[:], in_=zero[:], func=ACT.Exp)
+            make_identity(nc, ident[:])
+            nc.gpsimd.memset(ones[:], 1.0)
+
+            lg3 = lg[:].rearrange("p (t l) -> p t l", l=L)
+            mx_ = const.tile([P, NT], F32, name="mx_")
+            nc.vector.tensor_reduce(out=mx_[:], in_=lg3, axis=AX.X, op=ALU.max)
+            dd = const.tile([P, NT, L], F32, name="dd")
+            nc.vector.tensor_tensor(out=dd[:], in0=lg3, in1=mx_[:].unsqueeze(2).to_broadcast([P, NT, L]), op=ALU.subtract)
+            ee = const.tile([P, NT, L], F32, name="ee")
+            nc.scalar.activation(out=ee[:], in_=dd[:], func=ACT.Exp)
+            sm = const.tile([P, NT], F32, name="sm")
+            nc.vector.tensor_reduce(out=sm[:], in_=ee[:], axis=AX.X, op=ALU.add)
+            rs = const.tile([P, NT], F32, name="rs")
+            nc.vector.reciprocal(out=rs[:], in_=sm[:])
+            nc.vector.tensor_tensor(out=act[:], in0=ee[:], in1=rs[:].unsqueeze(2).to_broadcast([P, NT, L]), op=ALU.mult)
+
+            bps = bpp.tile([P, NC], F32, name="bps")
+            nc.tensor.matmul(out=bps[:], lhsT=ones[:], rhs=brow[:], start=True, stop=True)
+            nc.scalar.copy(out=bias[:], in_=bps[:])
+
+            def w_prep(g):
+                wg = wtmp.tile([P, NC * PACK], BF16, name="wg", align_bytes=64, bufs=2)
+                wgw = wg[:].bitcast(F32).rearrange("p (j r u) -> p j r u", j=NS, u=2)
+                for jj in (0, 2):
+                    xt = xtp.tile([P, 2, 2, P], F32, name="xt")
+                    for a in range(2):
+                        words = wraw[jj + a][:].bitcast(F32)
+                        for u in range(2):
+                            nc.tensor.transpose(out=xt[:, a, u, :], in_=words[:, 256 * g + u : 256 * (g + 1) : 2], identity=ident[:])
+                    nc.scalar.copy(out=wgw[:, jj : jj + 2, :, :], in_=xt[:].rearrange("p a u r -> p a r u"))
+                nc.vector.quantize_mx(out=wc[:, g * NC : (g + 1) * NC].bitcast(FP8X4), scales=ws[:, g * NC : (g + 1) * NC], in_=wg[:])
+
+            prod_rest(0, 1, 4)
+            prod_rest(0, 4, SS)
+            prod_rest(1)
+            for k in range(4):
+                prod_rest(k + 2)
+                if k == 0:
+                    t1(k, 1, 4)
+                    t1(k, 4, SS)
+                else:
+                    t1(k, 1, SS)
+                if k >= 1:
+                    t2(k - 1, 1, SS - 1)
+                if k == 1:
+                    w_prep(0)
+                    w_prep(1)
+                if k == 2:
+                    w_prep(2)
+                    w_prep(3)
+
+        late["qtp"] = ctx.enter_context(tc.tile_pool(name="qtp", bufs=3))
+        late["qp"] = ctx.enter_context(tc.tile_pool(name="qp", bufs=4))
+
+        for t in (0, 1):
+            h_trans(t)
+            h_quant(t)
+            mm(t)
+            badd(t)
+        for k in range(4, 6):
+            vprod_rest(k + 2)
+            t1(k, 1, SS)
+            t2(k - 1, 1, SS - 1)
+        tops([0, 1, 2, 3])
+        store0(0)
+        store0(1)
+        for t in (2, 3):
+            h_trans(t)
+            h_quant(t)
+            mm(t)
+        qprod(6, 1)
+        qprod(7, 1)
+        qprod(5, 1)
+
+        cast_q = [0, 1]
+        red_q = [2, 3]
+        with tc.manual_schedule(engines={ENG.DVE, ENG.Pool}):
+            t1(6, 1, SS)
+            t1(7, 1, SS)
+            gadd(6, 1)
+            gadd(7, 1)
+            gadd(5, 1)
+            red(0)
+            red(1)
+            badd(2)
+            badd(3)
+            rcp(0)
+            rcp(1)
+            tops([4, 5, 6, 7])
+            store0(2)
+            store0(3)
+            for k in (8, 10, 11, 9):
+                prod_rest(k)
+                prod_top(k)
+            h_trans(4)
+            qprod(9, 0)
+            qprod(10, 0)
+            qprod(11, 0)
+
+            for t in range(2, NT):
+                last = t == NT - 1
+                todo = list(cast_q)
+                cast_q.clear()
+                for m in todo:
+                    mul(m)
+                if not last:
+                    for k in range(NS * (t + 1), NS * (t + 2)):
+                        prod_rest(k)
+                        prod_top(k)
+                    qprod(NS * (t + 1) + 2, 0)
+                    qprod(NS * (t + 1) + 3, 0)
+                if t + 3 < NT:
+                    h_trans(t + 3)
+                if 2 < t < NT - 2:
+                    mm(t + 2)
+                for m in todo:
+                    scasts(m, CV_STEADY)
+                k0 = NS * t
+                if t == 2:
+                    t1(k0, 0, SS)
+                    t1(k0 + 2, 0, SS)
+                    t2(k0, 0, SS - 1)
+                    t1(k0 + 3, 0, SS)
+                    h_quant(4)
+                    mm(4)
+                    t1(k0 + 1, 0, SS)
+                    gadd(k0 + 1, 0)
+                    store0(2 * t)
+                else:
+                    t1(k0, 0, SS)
+                    t1(k0 + 1, 0, SS)
+                    t2(k0, 0, SS - 1)
+                    t2(k0 + 1, 0, SS - 1)
+                    store0(2 * t)
+                    t1(k0 + 2, 0, SS)
+                    t1(k0 + 3, 0, SS)
+                gadd(k0 + 2, 0)
+                gadd(k0 + 3, 0)
+                store0(2 * t + 1)
+                reds = red_q + [2 * t]
+                red_q = [2 * t + 1]
+                for m in reds:
+                    red(m)
+                if t + 2 < NT:
+                    badd(t + 2)
+                for m in reds:
+                    rcp(m)
+                    cast_q.append(m)
+                if t + 3 < NT:
+                    h_quant(t + 3)
+                for m in todo:
+                    vcasts(m, CV_STEADY)
+                    store1(m)
+
+            mlast = NH - 1
+            for m in cast_q:
+                mul(m)
+            red(mlast, 0, 1)
+            red(mlast, 1, 2)
+            for m in cast_q:
+                scasts(m, CV_TAIL[m])
+            for m in cast_q:
+                vcasts(m, CV_TAIL[m])
+                store1(m)
+            rcp(mlast)
+            vmul(mlast)
+            scasts(mlast, CV_LAST)
+            vcasts(mlast, SS)
+            store1(mlast, 0, SS)
+            vcasts(mlast, CV_LAST, SS)
+            store1(mlast, SS, HR)

@@ -19,6 +19,7 @@ OUT_BUFS = 8
 CV_STEADY = 0
 CV_TAIL = {13: 0, 14: 8}
 CV_LAST = 12
+GP = {2: 6, 3: 5, 4: 5, 5: 5, 6: 0, 7: 0}
 
 FLOPS = 2 * B * H * NC + 5 * B * NS * SS * CS
 
@@ -141,12 +142,20 @@ def tile_stackrnncore_pa_kernel(tc, h, act_logits, stacks, W_push, b_push, out_0
             t, n = divmod(k, NS)
             nc.scalar.activation(out=uo(k)[:, 0, :], in_=pbs[t][:, n * CS : (n + 1) * CS], func=ACT.Copy, scale=wgt(k, 0))
 
-        def qprod(k, lo):
+        def qprod(k, lo, hi=SS - 1):
             if k // 2 not in qts:
                 qt = late["qtp"].tile([P, 2, SS - 1, CS], F32, name="qt")
                 qts[k // 2] = qt
             sv = st[divmod(k, NS)]
-            nc.scalar.activation(out=qts[k // 2][:, k % 2, lo : SS - 1, :], in_=sv[:, lo + 1 : SS, :], func=ACT.Copy, scale=wgt(k, 1))
+            nc.scalar.activation(out=qts[k // 2][:, k % 2, lo:hi, :], in_=sv[:, lo + 1 : hi + 1, :], func=ACT.Copy, scale=wgt(k, 1))
+
+        def gprod(k, lo, hi=SS - 1):
+            sv = st[divmod(k, NS)]
+            nc.gpsimd.tensor_scalar(out=qts[k // 2][:, k % 2, lo:hi, :], in0=sv[:, lo + 1 : hi + 1, :], scalar1=wgt(k, 1), scalar2=0.0, op0=ALU.mult, op1=ALU.add)
+
+        def gadd2(m, lo):
+            o = os_[m]
+            nc.gpsimd.tensor_tensor(out=o[:, :, lo : SS - 1, :], in0=o[:, :, lo : SS - 1, :], in1=qts[m][:, :, lo : SS - 1, :], op=ALU.add)
 
         def gadd(k, lo):
             o = uo(k)
@@ -318,8 +327,7 @@ def tile_stackrnncore_pa_kernel(tc, h, act_logits, stacks, W_push, b_push, out_0
         with tc.manual_schedule(engines={ENG.DVE, ENG.Pool}):
             t1(6, 1, SS)
             t1(7, 1, SS)
-            gadd(6, 1)
-            gadd(7, 1)
+            gadd2(3, 1)
             gadd(5, 1)
             red(0)
             red(1)
@@ -349,7 +357,7 @@ def tile_stackrnncore_pa_kernel(tc, h, act_logits, stacks, W_push, b_push, out_0
                         prod_rest(k)
                         prod_top(k)
                     qprod(NS * (t + 1) + 2, 0)
-                    qprod(NS * (t + 1) + 3, 0)
+                    qprod(NS * (t + 1) + 3, 0, SS - 1 - GP[t])
                 if t + 3 < NT:
                     h_trans(t + 3)
                 if 2 < t < NT - 2:
@@ -375,9 +383,10 @@ def tile_stackrnncore_pa_kernel(tc, h, act_logits, stacks, W_push, b_push, out_0
                     store0(2 * t)
                     t1(k0 + 2, 0, SS)
                     t1(k0 + 3, 0, SS)
-                gadd(k0 + 2, 0)
-                gadd(k0 + 3, 0)
+                gadd2(2 * t + 1, 0)
                 store0(2 * t + 1)
+                if GP[t]:
+                    gprod(NS * (t + 1) + 3, SS - 1 - GP[t])
                 reds = red_q + [2 * t]
                 red_q = [2 * t + 1]
                 for m in reds:

@@ -19,7 +19,9 @@ OUT_BUFS = 8
 CV_STEADY = 0
 CV_TAIL = {13: 0, 14: 8}
 CV_LAST = 12
-GP = {2: 6, 3: 5, 4: 5, 5: 5, 6: 0, 7: 0}
+GP = {2: 0, 3: 4, 4: 4, 5: 4, 6: 0, 7: 0}
+G1 = {3: 3, 4: 3, 5: 3, 6: 4, 7: 0}
+G1MAX = 4
 
 FLOPS = 2 * B * H * NC + 5 * B * NS * SS * CS
 
@@ -53,7 +55,7 @@ def tile_stackrnncore_pa_kernel(tc, h, act_logits, stacks, W_push, b_push, out_0
         stat = ctx.enter_context(tc.tile_pool(name="stat", bufs=6))
         xtp = ctx.enter_context(tc.psum_pool(name="xtp", bufs=4))
         accp = ctx.enter_context(tc.psum_pool(name="accp", bufs=2))
-        bpp = ctx.enter_context(tc.psum_pool(name="bpp", bufs=1))
+        bpp = ctx.enter_context(tc.psum_pool(name="bpp", bufs=2))
 
         st = {}
         hraw = []
@@ -66,12 +68,15 @@ def tile_stackrnncore_pa_kernel(tc, h, act_logits, stacks, W_push, b_push, out_0
         stats = {}
         qs = {}
         late = {}
+        sps = {}
+        q1s = {}
 
         lg = const.tile([P, NT * L], BF16, name="lg")
         zero = const.tile([P, 1], F32, name="zero")
         warm = const.tile([P, 1], F32, name="warm")
         ident = const.tile([P, P], F32, name="ident")
         ones = const.tile([P, P], BF16, name="ones")
+        identb = const.tile([P, P], BF16, name="identb")
         brow = const.tile([P, NC], BF16, name="brow")
         bias = const.tile([P, NC], F32, name="bias")
         act = const.tile([P, NT, L], F32, name="act")
@@ -166,6 +171,29 @@ def tile_stackrnncore_pa_kernel(tc, h, act_logits, stacks, W_push, b_push, out_0
             sv = st[divmod(k, NS)]
             nc.vector.scalar_tensor_tensor(out=o[:, lo:hi, :], in0=sv[:, lo:hi, :], scalar=wgt(k, 2), in1=o[:, lo:hi, :], op0=ALU.mult, op1=ALU.add)
 
+        def spm(k):
+            sv = st[divmod(k, NS)]
+            sps[k] = []
+            for a in range(2):
+                sp = bpp.tile([P, NC], F32, name="sp")
+                nc.tensor.matmul(out=sp[:], lhsT=identb[:], rhs=sv[:, 4 * a : 4 * a + 4, :].rearrange("p i c -> p (i c)"), start=True, stop=True)
+                sps[k].append(sp)
+
+        def t1p(k):
+            o = uo(k)
+            for a in range(2):
+                nc.vector.scalar_tensor_tensor(out=o[:, 4 * a : 4 * a + 4, :], in0=sps[k][a][:].rearrange("p (i c) -> p i c", c=CS), scalar=wgt(k, 2), in1=o[:, 4 * a : 4 * a + 4, :], op0=ALU.mult, op1=ALU.add)
+
+        def q1prod(k, n):
+            q1 = late["q1p"].tile([P, G1MAX, CS], F32, name="q1")
+            q1s[k] = q1
+            sv = st[divmod(k, NS)]
+            nc.scalar.activation(out=q1[:, 0:n, :], in_=sv[:, SS - n : SS, :], func=ACT.Copy, scale=wgt(k, 1))
+
+        def gadd1(k, n):
+            o = uo(k)
+            nc.gpsimd.tensor_tensor(out=o[:, SS - 1 - n : SS - 1, :], in0=o[:, SS - 1 - n : SS - 1, :], in1=q1s[k][:, 0:n, :], op=ALU.add)
+
         def t2(k, lo, hi):
             o = uo(k)
             sv = st[divmod(k, NS)]
@@ -250,6 +278,7 @@ def tile_stackrnncore_pa_kernel(tc, h, act_logits, stacks, W_push, b_push, out_0
             nc.scalar.activation(out=warm[:], in_=zero[:], func=ACT.Exp)
             make_identity(nc, ident[:])
             nc.gpsimd.memset(ones[:], 1.0)
+            make_identity(nc, identb[:])
 
             lg3 = lg[:].rearrange("p (t l) -> p t l", l=L)
             mx_ = const.tile([P, NT], F32, name="mx_")
@@ -264,7 +293,7 @@ def tile_stackrnncore_pa_kernel(tc, h, act_logits, stacks, W_push, b_push, out_0
             nc.vector.reciprocal(out=rs[:], in_=sm[:])
             nc.vector.tensor_tensor(out=act[:], in0=ee[:], in1=rs[:].unsqueeze(2).to_broadcast([P, NT, L]), op=ALU.mult)
 
-            bps = bpp.tile([P, NC], F32, name="bps")
+            bps = bpp.tile([P, NC], F32, name="sp")
             nc.tensor.matmul(out=bps[:], lhsT=ones[:], rhs=brow[:], start=True, stop=True)
             nc.scalar.copy(out=bias[:], in_=bps[:])
 
@@ -301,6 +330,7 @@ def tile_stackrnncore_pa_kernel(tc, h, act_logits, stacks, W_push, b_push, out_0
 
         late["qtp"] = ctx.enter_context(tc.tile_pool(name="qtp", bufs=3))
         late["qp"] = ctx.enter_context(tc.tile_pool(name="qp", bufs=4))
+        late["q1p"] = ctx.enter_context(tc.tile_pool(name="q1p", bufs=2))
 
         for t in (0, 1):
             h_trans(t)
@@ -343,6 +373,7 @@ def tile_stackrnncore_pa_kernel(tc, h, act_logits, stacks, W_push, b_push, out_0
                 prod_top(k)
             h_trans(4)
             qprod(9, 0)
+            qprod(8, 0)
             qprod(10, 0)
             qprod(11, 0)
 
@@ -356,8 +387,11 @@ def tile_stackrnncore_pa_kernel(tc, h, act_logits, stacks, W_push, b_push, out_0
                     for k in range(NS * (t + 1), NS * (t + 2)):
                         prod_rest(k)
                         prod_top(k)
+                    if G1[t + 1]:
+                        q1prod(NS * (t + 1) + 1, G1[t + 1])
                     qprod(NS * (t + 1) + 2, 0)
                     qprod(NS * (t + 1) + 3, 0, SS - 1 - GP[t])
+                    spm(NS * (t + 1))
                 if t + 3 < NT:
                     h_trans(t + 3)
                 if 2 < t < NT - 2:
@@ -368,21 +402,21 @@ def tile_stackrnncore_pa_kernel(tc, h, act_logits, stacks, W_push, b_push, out_0
                 if t == 2:
                     t1(k0, 0, SS)
                     t1(k0 + 2, 0, SS)
-                    t2(k0, 0, SS - 1)
                     t1(k0 + 3, 0, SS)
                     h_quant(4)
                     mm(4)
                     t1(k0 + 1, 0, SS)
-                    gadd(k0 + 1, 0)
+                    gadd2(2 * t, 0)
                     store0(2 * t)
                 else:
-                    t1(k0, 0, SS)
-                    t1(k0 + 1, 0, SS)
                     t2(k0, 0, SS - 1)
-                    t2(k0 + 1, 0, SS - 1)
-                    store0(2 * t)
+                    t2(k0 + 1, 0, SS - 1 - G1[t])
                     t1(k0 + 2, 0, SS)
                     t1(k0 + 3, 0, SS)
+                    t1(k0 + 1, 0, SS)
+                    if G1[t]:
+                        gadd1(k0 + 1, G1[t])
+                    store0(2 * t)
                 gadd2(2 * t + 1, 0)
                 store0(2 * t + 1)
                 if GP[t]:
@@ -396,6 +430,8 @@ def tile_stackrnncore_pa_kernel(tc, h, act_logits, stacks, W_push, b_push, out_0
                 for m in reds:
                     rcp(m)
                     cast_q.append(m)
+                if not last:
+                    t1p(NS * (t + 1))
                 if t + 3 < NT:
                     h_quant(t + 3)
                 for m in todo:

@@ -19,9 +19,9 @@ OUT_BUFS = 8
 CV_STEADY = 0
 CV_TAIL = {13: 0, 14: 8}
 CV_LAST = 12
-GP = {2: 0, 3: 4, 4: 4, 5: 4, 6: 0, 7: 0}
-G1 = {3: 3, 4: 3, 5: 3, 6: 4, 7: 0}
-G1MAX = 4
+GP = {2: 0, 3: 5, 4: 5, 5: 5, 6: 7, 7: 0}
+G1 = {3: 2, 4: 2, 5: 2, 6: 0, 7: 0}
+G1MAX = 2
 
 FLOPS = 2 * B * H * NC + 5 * B * NS * SS * CS
 
@@ -390,7 +390,8 @@ def tile_stackrnncore_pa_kernel(tc, h, act_logits, stacks, W_push, b_push, out_0
                     if G1[t + 1]:
                         q1prod(NS * (t + 1) + 1, G1[t + 1])
                     qprod(NS * (t + 1) + 2, 0)
-                    qprod(NS * (t + 1) + 3, 0, SS - 1 - GP[t])
+                    if GP[t] < SS - 1:
+                        qprod(NS * (t + 1) + 3, 0, SS - 1 - GP[t])
                     spm(NS * (t + 1))
                 if t + 3 < NT:
                     h_trans(t + 3)

@@ -18,7 +18,7 @@ HR = 2 * SS
 OUT_BUFS = 8
 CV_STEADY = 0
 CV_TAIL = {13: 0, 14: 8}
-CV_LAST = 12
+CV_LAST = 14
 GP = {2: 0, 3: 5, 4: 5, 5: 5, 6: 7, 7: 0}
 G1 = {3: 2, 4: 2, 5: 2, 6: 0, 7: 0}
 G1MAX = 2
@@ -202,42 +202,45 @@ def tile_stackrnncore_pa_kernel(tc, h, act_logits, stacks, W_push, b_push, out_0
         def store0(m):
             nc.sync.dma_start(out=o0_v[:, m, :], in_=os_[m][:].rearrange("p b i c -> p (b i c)"))
 
-        def red(m, b0=0, b1=2):
-            if b0 == 0:
-                am = stat.tile([P, HR], F32, name="am")
-                rc = stat.tile([P, HR], F32, name="rc")
-                r4 = stat.tile([P, HR], F32, name="r4")
-                stats[m] = (am, rc, r4)
-            am = stats[m][0]
-            nc.vector.tensor_reduce(out=am[:, b0 * SS : b1 * SS], in_=os_[m][:, b0:b1, :, :].rearrange("p b i c -> p (b i) c"), axis=AX.X, op=ALU.max, apply_absolute_value=True)
+        def group(ms):
+            am = stat.tile([P, len(ms) * HR], F32, name="am")
+            rc = stat.tile([P, len(ms) * HR], F32, name="rc")
+            r4 = stat.tile([P, len(ms) * HR], F32, name="r4")
+            for g, m in enumerate(ms):
+                stats[m] = (am, rc, r4, g * HR)
 
-        def rcp(m):
-            am, rc, r4 = stats[m]
+        def red(m, b0=0, b1=2):
+            am, off = stats[m][0], stats[m][3]
+            nc.vector.tensor_reduce(out=am[:, off + b0 * SS : off + b1 * SS], in_=os_[m][:, b0:b1, :, :].rearrange("p b i c -> p (b i) c"), axis=AX.X, op=ALU.max, apply_absolute_value=True)
+
+        def rcp(ms):
+            am, rc = stats[ms[0]][0], stats[ms[0]][1]
             nc.vector.reciprocal(out=rc[:], in_=am[:])
 
-        def mul(m):
-            am, rc, r4 = stats[m]
+        def mul(ms):
+            rc, r4 = stats[ms[0]][1], stats[ms[0]][2]
             nc.scalar.activation(out=r4[:], in_=rc[:], func=ACT.Copy, scale=448.0)
-            q = late["qp"].tile([P, HR, CS], FP8, name="q")
-            qs[m] = q
+            for m in ms:
+                q = late["qp"].tile([P, HR, CS], FP8, name="q")
+                qs[m] = q
 
         def vmul(m):
-            am, rc, r4 = stats[m]
+            rc, r4 = stats[m][1], stats[m][2]
             nc.vector.tensor_scalar(out=r4[:], in0=rc[:], scalar1=448.0, scalar2=None, op0=ALU.mult)
             q = late["qp"].tile([P, HR, CS], FP8, name="q")
             qs[m] = q
 
         def scasts(m, cv):
-            r4 = stats[m][2]
+            r4, off = stats[m][2], stats[m][3]
             ov = os_[m][:].rearrange("p b i c -> p (b i) c")
             for j in range(cv, HR):
-                nc.scalar.activation(out=qs[m][:, j, :], in_=ov[:, j, :], func=ACT.Identity, scale=r4[:, j : j + 1], bias=zero[:, 0:1], saturate=False)
+                nc.scalar.activation(out=qs[m][:, j, :], in_=ov[:, j, :], func=ACT.Identity, scale=r4[:, off + j : off + j + 1], bias=zero[:, 0:1], saturate=False)
 
         def vcasts(m, cv, c0=0):
-            r4 = stats[m][2]
+            r4, off = stats[m][2], stats[m][3]
             ov = os_[m][:].rearrange("p b i c -> p (b i) c")
             for j in range(c0, cv):
-                nc.vector.tensor_scalar(out=qs[m][:, j, :], in0=ov[:, j, :], scalar1=r4[:, j : j + 1], scalar2=None, op0=ALU.mult, saturate=False)
+                nc.vector.tensor_scalar(out=qs[m][:, j, :], in0=ov[:, j, :], scalar1=r4[:, off + j : off + j + 1], scalar2=None, op0=ALU.mult, saturate=False)
 
         def store1(m, j0=0, j1=HR):
             nc.sync.dma_start(out=o1_v[:, m, j0 * CS : j1 * CS], in_=qs[m][:, j0:j1, :].bitcast(U8).rearrange("p j c -> p (j c)"))
@@ -359,12 +362,12 @@ def tile_stackrnncore_pa_kernel(tc, h, act_logits, stacks, W_push, b_push, out_0
             t1(7, 1, SS)
             gadd2(3, 1)
             gadd(5, 1)
+            group([0, 1])
             red(0)
             red(1)
             badd(2)
             badd(3)
-            rcp(0)
-            rcp(1)
+            rcp([0, 1])
             tops([4, 5, 6, 7])
             store0(2)
             store0(3)
@@ -381,8 +384,7 @@ def tile_stackrnncore_pa_kernel(tc, h, act_logits, stacks, W_push, b_push, out_0
                 last = t == NT - 1
                 todo = list(cast_q)
                 cast_q.clear()
-                for m in todo:
-                    mul(m)
+                mul(todo)
                 if not last:
                     for k in range(NS * (t + 1), NS * (t + 2)):
                         prod_rest(k)
@@ -424,13 +426,13 @@ def tile_stackrnncore_pa_kernel(tc, h, act_logits, stacks, W_push, b_push, out_0
                     gprod(NS * (t + 1) + 3, SS - 1 - GP[t])
                 reds = red_q + [2 * t]
                 red_q = [2 * t + 1]
+                group(reds)
                 for m in reds:
                     red(m)
                 if t + 2 < NT:
                     badd(t + 2)
-                for m in reds:
-                    rcp(m)
-                    cast_q.append(m)
+                rcp(reds)
+                cast_q.extend(reds)
                 if not last:
                     t1p(NS * (t + 1))
                 if t + 3 < NT:
@@ -440,8 +442,8 @@ def tile_stackrnncore_pa_kernel(tc, h, act_logits, stacks, W_push, b_push, out_0
                     store1(m)
 
             mlast = NH - 1
-            for m in cast_q:
-                mul(m)
+            mul(cast_q)
+            group([mlast])
             red(mlast, 0, 1)
             red(mlast, 1, 2)
             for m in cast_q:
@@ -449,7 +451,7 @@ def tile_stackrnncore_pa_kernel(tc, h, act_logits, stacks, W_push, b_push, out_0
             for m in cast_q:
                 vcasts(m, CV_TAIL[m])
                 store1(m)
-            rcp(mlast)
+            rcp([mlast])
             vmul(mlast)
             scasts(mlast, CV_LAST)
             vcasts(mlast, SS)

@@ -17,8 +17,8 @@ L = NS * NA
 HR = 2 * SS
 OUT_BUFS = 8
 CV_STEADY = 0
-CV_TAIL = {13: 0, 14: 8}
-CV_LAST = 14
+CV_TAIL = {13: 0, 14: 3}
+CV_LAST = 11
 GP = {2: 0, 3: 5, 4: 5, 5: 5, 6: 7, 7: 0}
 G1 = {3: 2, 4: 2, 5: 2, 6: 0, 7: 0}
 G1MAX = 2
@@ -426,12 +426,18 @@ def tile_stackrnncore_pa_kernel(tc, h, act_logits, stacks, W_push, b_push, out_0
                     gprod(NS * (t + 1) + 3, SS - 1 - GP[t])
                 reds = red_q + [2 * t]
                 red_q = [2 * t + 1]
-                group(reds)
-                for m in reds:
-                    red(m)
-                if t + 2 < NT:
-                    badd(t + 2)
-                rcp(reds)
+                if last:
+                    for m in reds:
+                        group([m])
+                        red(m)
+                        rcp([m])
+                else:
+                    group(reds)
+                    for m in reds:
+                        red(m)
+                    if t + 2 < NT:
+                        badd(t + 2)
+                    rcp(reds)
                 cast_q.extend(reds)
                 if not last:
                     t1p(NS * (t + 1))
@@ -442,7 +448,8 @@ def tile_stackrnncore_pa_kernel(tc, h, act_logits, stacks, W_push, b_push, out_0
                     store1(m)
 
             mlast = NH - 1
-            mul(cast_q)
+            for m in cast_q:
+                mul([m])
             group([mlast])
             red(mlast, 0, 1)
             red(mlast, 1, 2)

@@ -261,6 +261,13 @@ def tile_stackrnncore_pa_kernel(tc, h, act_logits, stacks, W_push, b_push, out_0
         nc.gpsimd.memset(brow[:], 0.0)
         nc.sync.dma_start(out=brow[0:1, :], in_=b_push.rearrange("(o n) -> o n", o=1))
 
+        def load_stacks(t):
+            s1 = const.tile([P, NS, UNIT], BF16, name="st%d" % t)
+            nc.sync.dma_start(out=s1[:], in_=st_v[:, t, :, :])
+            for n in range(NS):
+                st[(t, n)] = s1[:, n, :].rearrange("p (i c) -> p i c", c=CS)
+
+        load_stacks(1)
         with tc.tile_pool(name="wtmp", bufs=1) as wtmp:
             wraw = []
             for j in range(NS):
@@ -271,11 +278,8 @@ def tile_stackrnncore_pa_kernel(tc, h, act_logits, stacks, W_push, b_push, out_0
                 hr = const.tile([P, H], BF16, name="hraw%d" % t)
                 nc.sync.dma_start(out=hr[:], in_=h_v[:, t, :])
                 hraw.append(hr)
-                if t + 1 < NT:
-                    s1 = const.tile([P, NS, UNIT], BF16, name="st%d" % (t + 1))
-                    nc.sync.dma_start(out=s1[:], in_=st_v[:, t + 1, :, :])
-                    for n in range(NS):
-                        st[(t + 1, n)] = s1[:, n, :].rearrange("p (i c) -> p i c", c=CS)
+                if t >= 2:
+                    load_stacks(t)
 
             nc.vector.memset(zero[:], 0.0)
             nc.scalar.activation(out=warm[:], in_=zero[:], func=ACT.Exp)
@@ -296,61 +300,74 @@ def tile_stackrnncore_pa_kernel(tc, h, act_logits, stacks, W_push, b_push, out_0
             nc.vector.reciprocal(out=rs[:], in_=sm[:])
             nc.vector.tensor_tensor(out=act[:], in0=ee[:], in1=rs[:].unsqueeze(2).to_broadcast([P, NT, L]), op=ALU.mult)
 
-            bps = bpp.tile([P, NC], F32, name="sp")
-            nc.tensor.matmul(out=bps[:], lhsT=ones[:], rhs=brow[:], start=True, stop=True)
-            nc.scalar.copy(out=bias[:], in_=bps[:])
+            wgs = []
+            for g in range(NPASS):
+                wg = wtmp.tile([P, NC * PACK], BF16, name="wg%d" % g, align_bytes=64)
+                wgs.append(wg)
 
-            def w_prep(g):
-                wg = wtmp.tile([P, NC * PACK], BF16, name="wg", align_bytes=64, bufs=2)
-                wgw = wg[:].bitcast(F32).rearrange("p (j r u) -> p j r u", j=NS, u=2)
+            def w_turn(g, jj):
+                wgw = wgs[g][:].bitcast(F32).rearrange("p (j r u) -> p j r u", j=NS, u=2)
+                xt = xtp.tile([P, 2, 2, P], F32, name="xt")
+                for a in range(2):
+                    words = wraw[jj + a][:].bitcast(F32)
+                    for u in range(2):
+                        nc.tensor.transpose(out=xt[:, a, u, :], in_=words[:, 256 * g + u : 256 * (g + 1) : 2], identity=ident[:])
+                nc.scalar.copy(out=wgw[:, jj : jj + 2, :, :], in_=xt[:].rearrange("p a u r -> p a r u"))
+
+            def w_quant(g):
+                nc.vector.quantize_mx(out=wc[:, g * NC : (g + 1) * NC].bitcast(FP8X4), scales=ws[:, g * NC : (g + 1) * NC], in_=wgs[g][:])
+
+            with tc.manual_schedule(engines={ENG.DVE, ENG.Activation, ENG.PE}):
+                prod_rest(0, 1, 4)
+                prod_rest(0, 4, SS)
+                for k in range(1, 6):
+                    prod_rest(k)
+                bps = bpp.tile([P, NC], F32, name="sp")
+                nc.tensor.matmul(out=bps[:], lhsT=ones[:], rhs=brow[:], start=True, stop=True)
+                nc.scalar.copy(out=bias[:], in_=bps[:])
                 for jj in (0, 2):
-                    xt = xtp.tile([P, 2, 2, P], F32, name="xt")
-                    for a in range(2):
-                        words = wraw[jj + a][:].bitcast(F32)
-                        for u in range(2):
-                            nc.tensor.transpose(out=xt[:, a, u, :], in_=words[:, 256 * g + u : 256 * (g + 1) : 2], identity=ident[:])
-                    nc.scalar.copy(out=wgw[:, jj : jj + 2, :, :], in_=xt[:].rearrange("p a u r -> p a r u"))
-                nc.vector.quantize_mx(out=wc[:, g * NC : (g + 1) * NC].bitcast(FP8X4), scales=ws[:, g * NC : (g + 1) * NC], in_=wg[:])
-
-            prod_rest(0, 1, 4)
-            prod_rest(0, 4, SS)
-            prod_rest(1)
-            for k in range(4):
-                prod_rest(k + 2)
-                if k == 0:
-                    t1(k, 1, 4)
-                    t1(k, 4, SS)
-                else:
+                    for g in range(NPASS):
+                        w_turn(g, jj)
+                h_trans(0)
+                t1(0, 1, 4)
+                t1(0, 4, SS)
+                t1(1, 1, SS)
+                for k in range(2, 4):
+                    t2(k - 2, 1, SS - 1)
                     t1(k, 1, SS)
-                if k >= 1:
-                    t2(k - 1, 1, SS - 1)
-                if k == 1:
-                    w_prep(0)
-                    w_prep(1)
-                if k == 2:
-                    w_prep(2)
-                    w_prep(3)
+                t2(2, 1, SS - 1)
+                t2(3, 1, SS - 1)
+                vprod_rest(6)
+                t1(4, 1, SS)
+                w_quant(0)
+                w_quant(1)
+                t2(4, 1, SS - 1)
+                w_quant(2)
+                w_quant(3)
+                h_quant(0)
 
         late["qtp"] = ctx.enter_context(tc.tile_pool(name="qtp", bufs=3))
         late["qp"] = ctx.enter_context(tc.tile_pool(name="qp", bufs=4))
         late["q1p"] = ctx.enter_context(tc.tile_pool(name="q1p", bufs=2))
 
-        for t in (0, 1):
-            h_trans(t)
-            h_quant(t)
-            mm(t)
-            badd(t)
-        for k in range(4, 6):
-            vprod_rest(k + 2)
-            t1(k, 1, SS)
-            t2(k - 1, 1, SS - 1)
-        tops([0, 1, 2, 3])
+        with tc.manual_schedule(engines={ENG.DVE, ENG.Activation, ENG.PE}):
+            h_trans(1)
+            mm(0)
+            vprod_rest(7)
+            t1(5, 1, SS)
+            h_quant(1)
+            h_trans(2)
+            mm(1)
+            badd(0)
+            tops([0, 1, 2, 3])
+            badd(1)
+            h_quant(2)
+            h_trans(3)
+            mm(2)
+            h_quant(3)
+            mm(3)
         store0(0)
         store0(1)
-        for t in (2, 3):
-            h_trans(t)
-            h_quant(t)
-            mm(t)
         qprod(6, 1)
         qprod(7, 1)
         qprod(5, 1)

@@ -17,8 +17,8 @@ L = NS * NA
 HR = 2 * SS
 OUT_BUFS = 8
 CV_STEADY = 0
-CV_TAIL = {13: 0, 14: 3}
-CV_LAST = 11
+CV_TAIL = {13: 0, 14: 6}
+CV_LAST = 12
 GP = {2: 0, 3: 5, 4: 5, 5: 5, 6: 7, 7: 0}
 G1 = {3: 2, 4: 2, 5: 2, 6: 0, 7: 0}
 G1MAX = 2
@@ -70,6 +70,7 @@ def tile_stackrnncore_pa_kernel(tc, h, act_logits, stacks, W_push, b_push, out_0
         late = {}
         sps = {}
         q1s = {}
+        hxs = {}
 
         lg = const.tile([P, NT * L], BF16, name="lg")
         zero = const.tile([P, 1], F32, name="zero")
@@ -90,9 +91,8 @@ def tile_stackrnncore_pa_kernel(tc, h, act_logits, stacks, W_push, b_push, out_0
         def uo(k):
             return os_[k // 2][:, k % 2, :, :]
 
-        def h_trans(t):
-            hg = hgp.tile([P, NPASS * P * PACK], BF16, name="hg", align_bytes=64)
-            hgw = hg[:].bitcast(F32).rearrange("p (g r u) -> p g r u", g=NPASS, u=2)
+        def h_turn(t):
+            hxs[t] = []
             words = hraw[t][:].bitcast(F32)
             for gg in (0, 2):
                 xt = xtp.tile([P, 2, 2, P], F32, name="xt")
@@ -100,8 +100,18 @@ def tile_stackrnncore_pa_kernel(tc, h, act_logits, stacks, W_push, b_push, out_0
                     g = gg + a
                     for u in range(2):
                         nc.tensor.transpose(out=xt[:, a, u, :], in_=words[:, 256 * g + u : 256 * (g + 1) : 2], identity=ident[:])
-                nc.scalar.copy(out=hgw[:, gg : gg + 2, :, :], in_=xt[:].rearrange("p a u r -> p a r u"))
+                hxs[t].append(xt)
+
+        def h_copy(t):
+            hg = hgp.tile([P, NPASS * P * PACK], BF16, name="hg", align_bytes=64)
+            hgw = hg[:].bitcast(F32).rearrange("p (g r u) -> p g r u", g=NPASS, u=2)
+            for i, xt in enumerate(hxs[t]):
+                nc.scalar.copy(out=hgw[:, 2 * i : 2 * i + 2, :, :], in_=xt[:].rearrange("p a u r -> p a r u"))
             hgs[t] = hg
+
+        def h_trans(t):
+            h_turn(t)
+            h_copy(t)
 
         def h_quant(t):
             hc = hcp.tile([P, NPASS * P], U32, name="hc", align_bytes=64)
@@ -253,6 +263,8 @@ def tile_stackrnncore_pa_kernel(tc, h, act_logits, stacks, W_push, b_push, out_0
             for k in ks:
                 t2(k, 0, 1)
 
+        ctx.enter_context(tc.manual_schedule(engines={ENG.DVE, ENG.Pool, ENG.Activation, ENG.PE}))
+
         nc.sync.dma_start(out=lg[:], in_=lg_v)
         for n in range(NS):
             s0 = const.tile([P, UNIT], BF16, name="st0_%d" % n)
@@ -317,168 +329,172 @@ def tile_stackrnncore_pa_kernel(tc, h, act_logits, stacks, W_push, b_push, out_0
             def w_quant(g):
                 nc.vector.quantize_mx(out=wc[:, g * NC : (g + 1) * NC].bitcast(FP8X4), scales=ws[:, g * NC : (g + 1) * NC], in_=wgs[g][:])
 
-            with tc.manual_schedule(engines={ENG.DVE, ENG.Activation, ENG.PE}):
-                prod_rest(0, 1, 4)
-                prod_rest(0, 4, SS)
-                for k in range(1, 6):
-                    prod_rest(k)
-                bps = bpp.tile([P, NC], F32, name="sp")
-                nc.tensor.matmul(out=bps[:], lhsT=ones[:], rhs=brow[:], start=True, stop=True)
-                nc.scalar.copy(out=bias[:], in_=bps[:])
-                for jj in (0, 2):
-                    for g in range(NPASS):
-                        w_turn(g, jj)
-                h_trans(0)
-                t1(0, 1, 4)
-                t1(0, 4, SS)
-                t1(1, 1, SS)
-                for k in range(2, 4):
-                    t2(k - 2, 1, SS - 1)
-                    t1(k, 1, SS)
-                t2(2, 1, SS - 1)
-                t2(3, 1, SS - 1)
-                vprod_rest(6)
-                t1(4, 1, SS)
-                w_quant(0)
-                w_quant(1)
-                t2(4, 1, SS - 1)
-                w_quant(2)
-                w_quant(3)
-                h_quant(0)
+            prod_rest(0, 1, 4)
+            prod_rest(0, 4, SS)
+            for k in range(1, 6):
+                prod_rest(k)
+            bps = bpp.tile([P, NC], F32, name="sp")
+            nc.tensor.matmul(out=bps[:], lhsT=ones[:], rhs=brow[:], start=True, stop=True)
+            nc.scalar.copy(out=bias[:], in_=bps[:])
+            for jj in (0, 2):
+                for g in range(NPASS):
+                    w_turn(g, jj)
+            h_turn(0)
+            h_copy(0)
+            t1(0, 1, 4)
+            t1(0, 4, SS)
+            t1(1, 1, SS)
+            for k in range(2, 4):
+                t2(k - 2, 1, SS - 1)
+                t1(k, 1, SS)
+            t2(2, 1, SS - 1)
+            t2(3, 1, SS - 1)
+            vprod_rest(6)
+            t1(4, 1, SS)
+            w_quant(0)
+            w_quant(1)
+            w_quant(2)
+            w_quant(3)
+            vprod_rest(7)
+            t1(5, 1, SS)
+            h_quant(0)
 
         late["qtp"] = ctx.enter_context(tc.tile_pool(name="qtp", bufs=3))
         late["qp"] = ctx.enter_context(tc.tile_pool(name="qp", bufs=4))
         late["q1p"] = ctx.enter_context(tc.tile_pool(name="q1p", bufs=2))
 
-        with tc.manual_schedule(engines={ENG.DVE, ENG.Activation, ENG.PE}):
-            h_trans(1)
-            mm(0)
-            vprod_rest(7)
-            t1(5, 1, SS)
-            h_quant(1)
-            h_trans(2)
-            mm(1)
-            badd(0)
-            tops([0, 1, 2, 3])
-            badd(1)
-            h_quant(2)
-            h_trans(3)
-            mm(2)
-            h_quant(3)
-            mm(3)
-        store0(0)
-        store0(1)
+        h_turn(1)
+        prod_rest(8)
+        h_copy(1)
+        t1(6, 1, SS)
+        h_quant(1)
+        t2(4, 1, SS - 1)
+        t1(8, 1, SS)
+        mm(0)
+        h_turn(2)
+        prod_rest(10)
         qprod(6, 1)
+        badd(0)
+        tops([0, 1, 2, 3])
+        h_turn(3)
+        mm(1)
+        h_copy(2)
+        h_copy(3)
+        h_quant(2)
+        h_quant(3)
+        mm(2)
         qprod(7, 1)
         qprod(5, 1)
+        prod_rest(11)
+        prod_rest(9)
+        store0(0)
+        store0(1)
 
         cast_q = [0, 1]
         red_q = [2, 3]
-        with tc.manual_schedule(engines={ENG.DVE, ENG.Pool}):
-            t1(6, 1, SS)
-            t1(7, 1, SS)
-            gadd2(3, 1)
-            gadd(5, 1)
-            group([0, 1])
-            red(0)
-            red(1)
-            badd(2)
-            badd(3)
-            rcp([0, 1])
-            tops([4, 5, 6, 7])
-            store0(2)
-            store0(3)
-            for k in (8, 10, 11, 9):
-                prod_rest(k)
-                prod_top(k)
-            h_trans(4)
-            qprod(9, 0)
-            qprod(8, 0)
-            qprod(10, 0)
-            qprod(11, 0)
+        t1(7, 1, SS)
+        mm(3)
+        gadd2(3, 1)
+        gadd(5, 1)
+        group([0, 1])
+        red(0)
+        badd(1)
+        red(1)
+        badd(2)
+        badd(3)
+        rcp([0, 1])
+        tops([4, 5, 6, 7])
+        store0(2)
+        store0(3)
+        for k in (8, 10, 11, 9):
+            prod_top(k)
+        h_trans(4)
+        qprod(9, 0)
+        qprod(8, 0)
+        qprod(10, 0)
+        qprod(11, 0)
 
-            for t in range(2, NT):
-                last = t == NT - 1
-                todo = list(cast_q)
-                cast_q.clear()
-                mul(todo)
-                if not last:
-                    for k in range(NS * (t + 1), NS * (t + 2)):
-                        prod_rest(k)
-                        prod_top(k)
-                    if G1[t + 1]:
-                        q1prod(NS * (t + 1) + 1, G1[t + 1])
-                    qprod(NS * (t + 1) + 2, 0)
-                    if GP[t] < SS - 1:
-                        qprod(NS * (t + 1) + 3, 0, SS - 1 - GP[t])
-                    spm(NS * (t + 1))
-                if t + 3 < NT:
-                    h_trans(t + 3)
-                if 2 < t < NT - 2:
-                    mm(t + 2)
-                for m in todo:
-                    scasts(m, CV_STEADY)
-                k0 = NS * t
-                if t == 2:
-                    t1(k0, 0, SS)
-                    t1(k0 + 2, 0, SS)
-                    t1(k0 + 3, 0, SS)
-                    h_quant(4)
-                    mm(4)
-                    t1(k0 + 1, 0, SS)
-                    gadd2(2 * t, 0)
-                    store0(2 * t)
-                else:
-                    t2(k0, 0, SS - 1)
-                    t2(k0 + 1, 0, SS - 1 - G1[t])
-                    t1(k0 + 2, 0, SS)
-                    t1(k0 + 3, 0, SS)
-                    t1(k0 + 1, 0, SS)
-                    if G1[t]:
-                        gadd1(k0 + 1, G1[t])
-                    store0(2 * t)
-                gadd2(2 * t + 1, 0)
-                store0(2 * t + 1)
-                if GP[t]:
-                    gprod(NS * (t + 1) + 3, SS - 1 - GP[t])
-                reds = red_q + [2 * t]
-                red_q = [2 * t + 1]
-                if last:
-                    for m in reds:
-                        group([m])
-                        red(m)
-                        rcp([m])
-                else:
-                    group(reds)
-                    for m in reds:
-                        red(m)
-                    if t + 2 < NT:
-                        badd(t + 2)
-                    rcp(reds)
-                cast_q.extend(reds)
-                if not last:
-                    t1p(NS * (t + 1))
-                if t + 3 < NT:
-                    h_quant(t + 3)
-                for m in todo:
-                    vcasts(m, CV_STEADY)
-                    store1(m)
-
-            mlast = NH - 1
-            for m in cast_q:
-                mul([m])
-            group([mlast])
-            red(mlast, 0, 1)
-            red(mlast, 1, 2)
-            for m in cast_q:
-                scasts(m, CV_TAIL[m])
-            for m in cast_q:
-                vcasts(m, CV_TAIL[m])
+        for t in range(2, NT):
+            last = t == NT - 1
+            todo = list(cast_q)
+            cast_q.clear()
+            mul(todo)
+            if not last:
+                for k in range(NS * (t + 1), NS * (t + 2)):
+                    prod_rest(k)
+                    prod_top(k)
+                    if k % NS == 1 and t + 3 < NT:
+                        h_trans(t + 3)
+                if G1[t + 1]:
+                    q1prod(NS * (t + 1) + 1, G1[t + 1])
+                qprod(NS * (t + 1) + 2, 0)
+                if GP[t] < SS - 1:
+                    qprod(NS * (t + 1) + 3, 0, SS - 1 - GP[t])
+                spm(NS * (t + 1))
+            if 2 < t < NT - 2:
+                mm(t + 2)
+            for m in todo:
+                scasts(m, CV_STEADY)
+            k0 = NS * t
+            if t == 2:
+                t1(k0, 0, 1)
+                t1(k0 + 2, 0, SS)
+                t1(k0 + 3, 0, SS)
+                h_quant(4)
+                mm(4)
+                t1(k0 + 1, 0, SS)
+                gadd2(2 * t, 0)
+                store0(2 * t)
+            else:
+                t2(k0, 0, SS - 1)
+                t2(k0 + 1, 0, SS - 1 - G1[t])
+                t1(k0 + 2, 0, SS)
+                t1(k0 + 3, 0, SS)
+                t1(k0 + 1, 0, SS)
+                if G1[t]:
+                    gadd1(k0 + 1, G1[t])
+                store0(2 * t)
+            gadd2(2 * t + 1, 0)
+            store0(2 * t + 1)
+            if GP[t]:
+                gprod(NS * (t + 1) + 3, SS - 1 - GP[t])
+            reds = red_q + [2 * t]
+            red_q = [2 * t + 1]
+            if last:
+                for m in reds:
+                    group([m])
+                    red(m)
+                    rcp([m])
+            else:
+                group(reds)
+                for m in reds:
+                    red(m)
+                if t + 2 < NT:
+                    badd(t + 2)
+                rcp(reds)
+            cast_q.extend(reds)
+            if not last:
+                t1p(NS * (t + 1))
+            if t + 3 < NT:
+                h_quant(t + 3)
+            for m in todo:
+                vcasts(m, CV_STEADY)
                 store1(m)
-            rcp([mlast])
-            vmul(mlast)
-            scasts(mlast, CV_LAST)
-            vcasts(mlast, SS)
-            store1(mlast, 0, SS)
-            vcasts(mlast, CV_LAST, SS)
-            store1(mlast, SS, HR)
+
+        mlast = NH - 1
+        group([mlast])
+        red(mlast, 0, 1)
+        red(mlast, 1, 2)
+        for m in cast_q:
+            mul([m])
+            scasts(m, CV_TAIL[m])
+        for m in cast_q:
+            vcasts(m, CV_TAIL[m])
+            store1(m)
+        rcp([mlast])
+        vmul(mlast)
+        scasts(mlast, CV_LAST)
+        vcasts(mlast, SS)
+        store1(mlast, 0, SS)
+        vcasts(mlast, CV_LAST, SS)
+        store1(mlast, SS, HR)

@@ -20,8 +20,8 @@ CV_STEADY = 0
 CV_TAIL = {13: 0, 14: 6}
 CV_LAST = 12
 GP = {2: 0, 3: 5, 4: 5, 5: 5, 6: 7, 7: 0}
-G1 = {3: 2, 4: 2, 5: 2, 6: 0, 7: 0}
-G1MAX = 2
+G1 = {3: 4, 4: 4, 5: 4, 6: 0, 7: 0}
+G1MAX = 4
 
 FLOPS = 2 * B * H * NC + 5 * B * NS * SS * CS
 
@@ -52,6 +52,7 @@ def tile_stackrnncore_pa_kernel(tc, h, act_logits, stacks, W_push, b_push, out_0
         hcp = ctx.enter_context(tc.tile_pool(name="hcp", bufs=3))
         pbp = ctx.enter_context(tc.tile_pool(name="pbp", bufs=3))
         outp = ctx.enter_context(tc.tile_pool(name="outp", bufs=OUT_BUFS))
+        topp = ctx.enter_context(tc.tile_pool(name="topp", bufs=1))
         stat = ctx.enter_context(tc.tile_pool(name="stat", bufs=6))
         xtp = ctx.enter_context(tc.psum_pool(name="xtp", bufs=4))
         accp = ctx.enter_context(tc.psum_pool(name="accp", bufs=2))
@@ -70,6 +71,10 @@ def tile_stackrnncore_pa_kernel(tc, h, act_logits, stacks, W_push, b_push, out_0
         late = {}
         sps = {}
         q1s = {}
+        topa = {}
+        topc = {}
+        topb = {}
+        topx = {}
         hxs = {}
 
         lg = const.tile([P, NT * L], BF16, name="lg")
@@ -156,6 +161,41 @@ def tile_stackrnncore_pa_kernel(tc, h, act_logits, stacks, W_push, b_push, out_0
         def prod_top(k):
             t, n = divmod(k, NS)
             nc.scalar.activation(out=uo(k)[:, 0, :], in_=pbs[t][:, n * CS : (n + 1) * CS], func=ACT.Copy, scale=wgt(k, 0))
+
+        def top_pops(t):
+            c = topp.tile([P, NS, CS], F32, name="topc")
+            for n in range(NS):
+                nc.scalar.activation(out=c[:, n, :], in_=st[(t, n)][:, 1, :], func=ACT.Copy, scale=wgt(NS * t + n, 1))
+            topc[t] = c
+
+        def top_pushes(t):
+            a = topp.tile([P, NS, CS], F32, name="topa")
+            for n in range(NS):
+                nc.scalar.activation(out=a[:, n, :], in_=pbs[t][:, n * CS : (n + 1) * CS], func=ACT.Copy, scale=wgt(NS * t + n, 0))
+            topa[t] = a
+
+        def top_sum(t):
+            b = xtp.tile([P, NS, CS], F32, name="xt")
+            for n in range(NS):
+                nc.tensor.matmul(out=b[:, n, :], lhsT=topa[t][:, n, :], rhs=ident[:], is_transpose=True, start=True, stop=False)
+                nc.tensor.matmul(out=b[:, n, :], lhsT=topc[t][:, n, :], rhs=ident[:], is_transpose=True, start=False, stop=True)
+            topb[t] = b
+
+        def top_copy(t):
+            x = topp.tile([P, NS, CS], F32, name="topx")
+            nc.scalar.copy(out=x[:], in_=topb[t][:])
+            topx[t] = x
+
+        def top_back(t):
+            b = xtp.tile([P, NS, CS], F32, name="xt")
+            for n in range(NS):
+                nc.tensor.transpose(out=b[:, n, :], in_=topx[t][:, n, :], identity=ident[:])
+            topb[t] = b
+
+        def top_last(t):
+            for n in range(NS):
+                k = NS * t + n
+                nc.vector.scalar_tensor_tensor(out=uo(k)[:, 0, :], in0=st[(t, n)][:, 0, :], scalar=wgt(k, 2), in1=topb[t][:, n, :], op0=ALU.mult, op1=ALU.add)
 
         def qprod(k, lo, hi=SS - 1):
             if k // 2 not in qts:
@@ -333,6 +373,7 @@ def tile_stackrnncore_pa_kernel(tc, h, act_logits, stacks, W_push, b_push, out_0
             prod_rest(0, 4, SS)
             for k in range(1, 6):
                 prod_rest(k)
+            top_pops(0)
             bps = bpp.tile([P, NC], F32, name="sp")
             nc.tensor.matmul(out=bps[:], lhsT=ones[:], rhs=brow[:], start=True, stop=True)
             nc.scalar.copy(out=bias[:], in_=bps[:])
@@ -351,54 +392,59 @@ def tile_stackrnncore_pa_kernel(tc, h, act_logits, stacks, W_push, b_push, out_0
             t2(3, 1, SS - 1)
             vprod_rest(6)
             t1(4, 1, SS)
-            w_quant(0)
-            w_quant(1)
-            w_quant(2)
-            w_quant(3)
-            vprod_rest(7)
+            for g in range(NPASS):
+                w_quant(g)
             t1(5, 1, SS)
             h_quant(0)
 
         late["qtp"] = ctx.enter_context(tc.tile_pool(name="qtp", bufs=3))
         late["qp"] = ctx.enter_context(tc.tile_pool(name="qp", bufs=4))
-        late["q1p"] = ctx.enter_context(tc.tile_pool(name="q1p", bufs=2))
+        late["q1p"] = ctx.enter_context(tc.tile_pool(name="q1p", bufs=1))
 
         h_turn(1)
-        prod_rest(8)
         h_copy(1)
         t1(6, 1, SS)
-        h_quant(1)
         t2(4, 1, SS - 1)
-        t1(8, 1, SS)
+        h_quant(1)
         mm(0)
+        prod_rest(8)
+        t1(8, 1, SS)
         h_turn(2)
         prod_rest(10)
-        qprod(6, 1)
         badd(0)
-        tops([0, 1, 2, 3])
-        h_turn(3)
-        mm(1)
         h_copy(2)
+        top_pushes(0)
+        h_turn(3)
+        top_sum(0)
         h_copy(3)
+        top_copy(0)
+        vprod_rest(7)
+        t1(10, 1, SS)
         h_quant(2)
+        mm(1)
+        top_back(0)
         h_quant(3)
         mm(2)
-        qprod(7, 1)
-        qprod(5, 1)
+        for k in (6, 7, 5):
+            qprod(k, 1)
+        t1(7, 1, SS)
         prod_rest(11)
         prod_rest(9)
-        store0(0)
-        store0(1)
+        qprod(9, 0)
+        qprod(8, 0)
 
         cast_q = [0, 1]
         red_q = [2, 3]
-        t1(7, 1, SS)
-        mm(3)
         gadd2(3, 1)
         gadd(5, 1)
+        top_last(0)
+        store0(0)
+        store0(1)
         group([0, 1])
         red(0)
         badd(1)
+        mm(3)
+        h_turn(4)
         red(1)
         badd(2)
         badd(3)
@@ -408,9 +454,7 @@ def tile_stackrnncore_pa_kernel(tc, h, act_logits, stacks, W_push, b_push, out_0
         store0(3)
         for k in (8, 10, 11, 9):
             prod_top(k)
-        h_trans(4)
-        qprod(9, 0)
-        qprod(8, 0)
+        h_copy(4)
         qprod(10, 0)
         qprod(11, 0)
 
@@ -425,8 +469,6 @@ def tile_stackrnncore_pa_kernel(tc, h, act_logits, stacks, W_push, b_push, out_0
                     prod_top(k)
                     if k % NS == 1 and t + 3 < NT:
                         h_trans(t + 3)
-                if G1[t + 1]:
-                    q1prod(NS * (t + 1) + 1, G1[t + 1])
                 qprod(NS * (t + 1) + 2, 0)
                 if GP[t] < SS - 1:
                     qprod(NS * (t + 1) + 3, 0, SS - 1 - GP[t])
@@ -438,7 +480,7 @@ def tile_stackrnncore_pa_kernel(tc, h, act_logits, stacks, W_push, b_push, out_0
             k0 = NS * t
             if t == 2:
                 t1(k0, 0, 1)
-                t1(k0 + 2, 0, SS)
+                t1(k0 + 2, 0, 1)
                 t1(k0 + 3, 0, SS)
                 h_quant(4)
                 mm(4)
@@ -477,6 +519,8 @@ def tile_stackrnncore_pa_kernel(tc, h, act_logits, stacks, W_push, b_push, out_0
                 t1p(NS * (t + 1))
             if t + 3 < NT:
                 h_quant(t + 3)
+            if not last and G1[t + 1]:
+                q1prod(NS * (t + 1) + 1, G1[t + 1])
             for m in todo:
                 vcasts(m, CV_STEADY)
                 store1(m)

from contextlib import ExitStack

import concourse.mybir as mybir
from concourse.masks import make_identity

B, H, NS, SS, CS, NA = 1024, 2048, 4, 8, 128, 3
NC = NS * CS
P = 128
NT = B // P
PACK = 4
K_PASS = P * PACK
NPASS = H // K_PASS
UNIT = SS * CS
NU = NT * NS
NH = NT * 2
L = NS * NA
HR = 2 * SS
OUT_BUFS = 8
CV_STEADY = 0
CV_TAIL = {13: 0, 14: 6}
CV_LAST = 12
GP = {2: 0, 3: 5, 4: 5, 5: 5, 6: 7, 7: 0}
G1 = {3: 4, 4: 4, 5: 4, 6: 0, 7: 0}
G1MAX = 4

FLOPS = 2 * B * H * NC + 5 * B * NS * SS * CS

F32 = mybir.dt.float32
BF16 = mybir.dt.bfloat16
U32 = mybir.dt.uint32
U8 = mybir.dt.uint8
FP8X4 = mybir.dt.float8_e4m3fn_x4
FP8 = mybir.dt.float8_e4m3fn
ALU = mybir.AluOpType
ACT = mybir.ActivationFunctionType
AX = mybir.AxisListType
ENG = mybir.EngineType


def tile_stackrnncore_pa_kernel(tc, h, act_logits, stacks, W_push, b_push, out_0, out_1):
    nc = tc.nc
    h_v = h.rearrange("(p t) k -> p t k", t=NT)
    lg_v = act_logits.rearrange("(p t) l -> p (t l)", t=NT)
    st_v = stacks.rearrange("(p t) n i c -> p t n (i c)", t=NT)
    w_v = W_push.rearrange("(j r) k -> r j k", r=P)
    o0_v = out_0.rearrange("(p t) (a b) i c -> p (t a) (b i c)", t=NT, a=2)
    o1_v = out_1.rearrange("(p t) (a b) i c -> p (t a) (b i c)", t=NT, a=2)

    with ExitStack() as ctx:
        const = ctx.enter_context(tc.tile_pool(name="const", bufs=1))
        hgp = ctx.enter_context(tc.tile_pool(name="hgp", bufs=2))
        hcp = ctx.enter_context(tc.tile_pool(name="hcp", bufs=3))
        pbp = ctx.enter_context(tc.tile_pool(name="pbp", bufs=3))
        outp = ctx.enter_context(tc.tile_pool(name="outp", bufs=OUT_BUFS))
        topp = ctx.enter_context(tc.tile_pool(name="topp", bufs=1))
        stat = ctx.enter_context(tc.tile_pool(name="stat", bufs=6))
        xtp = ctx.enter_context(tc.psum_pool(name="xtp", bufs=4))
        accp = ctx.enter_context(tc.psum_pool(name="accp", bufs=2))
        bpp = ctx.enter_context(tc.psum_pool(name="bpp", bufs=2))

        st = {}
        hraw = []
        hgs = {}
        hq = {}
        accs = {}
        pbs = {}
        os_ = {}
        qts = {}
        stats = {}
        qs = {}
        late = {}
        sps = {}
        q1s = {}
        topa = {}
        topc = {}
        topb = {}
        topx = {}
        hxs = {}

        lg = const.tile([P, NT * L], BF16, name="lg")
        zero = const.tile([P, 1], F32, name="zero")
        warm = const.tile([P, 1], F32, name="warm")
        ident = const.tile([P, P], F32, name="ident")
        ones = const.tile([P, P], BF16, name="ones")
        identb = const.tile([P, P], BF16, name="identb")
        brow = const.tile([P, NC], BF16, name="brow")
        bias = const.tile([P, NC], F32, name="bias")
        act = const.tile([P, NT, L], F32, name="act")
        wc = const.tile([P, NPASS * NC], U32, name="wc", align_bytes=64)
        ws = const.tile([P, NPASS * NC], U8, name="ws", align_bytes=64)

        def wgt(k, a):
            t, n = divmod(k, NS)
            return act[:, t, NA * n + a : NA * n + a + 1]

        def uo(k):
            return os_[k // 2][:, k % 2, :, :]

        def h_turn(t):
            hxs[t] = []
            words = hraw[t][:].bitcast(F32)
            for gg in (0, 2):
                xt = xtp.tile([P, 2, 2, P], F32, name="xt")
                for a in range(2):
                    g = gg + a
                    for u in range(2):
                        nc.tensor.transpose(out=xt[:, a, u, :], in_=words[:, 256 * g + u : 256 * (g + 1) : 2], identity=ident[:])
                hxs[t].append(xt)

        def h_copy(t):
            hg = hgp.tile([P, NPASS * P * PACK], BF16, name="hg", align_bytes=64)
            hgw = hg[:].bitcast(F32).rearrange("p (g r u) -> p g r u", g=NPASS, u=2)
            for i, xt in enumerate(hxs[t]):
                nc.scalar.copy(out=hgw[:, 2 * i : 2 * i + 2, :, :], in_=xt[:].rearrange("p a u r -> p a r u"))
            hgs[t] = hg

        def h_trans(t):
            h_turn(t)
            h_copy(t)

        def h_quant(t):
            hc = hcp.tile([P, NPASS * P], U32, name="hc", align_bytes=64)
            hs = hcp.tile([P, NPASS * P], U8, name="hs", align_bytes=64)
            nc.vector.quantize_mx(out=hc[:].bitcast(FP8X4), scales=hs[:], in_=hgs[t][:])
            hq[t] = (hc, hs)

        def mm(t):
            hc, hs = hq[t]
            acc = accp.tile([P, NC], F32, name="acc")
            for g in range(NPASS):
                nc.tensor.matmul_mx(
                    out=acc[:],
                    lhsT=hc[:, g * P : (g + 1) * P].bitcast(FP8X4),
                    lhsT_scale=hs[:, g * P : (g + 1) * P],
                    rhs=wc[:, g * NC : (g + 1) * NC].bitcast(FP8X4),
                    rhs_scale=ws[:, g * NC : (g + 1) * NC],
                    start=(g == 0),
                    stop=(g == NPASS - 1),
                )
            accs[t] = acc

        def badd(t):
            pb = pbp.tile([P, NC], F32, name="pb")
            nc.vector.tensor_tensor(out=pb[:], in0=accs[t][:], in1=bias[:], op=ALU.add)
            pbs[t] = pb

        def prod_rest(k, lo=1, hi=SS):
            if k // 2 not in os_:
                o = outp.tile([P, 2, SS, CS], F32, name="o")
                os_[k // 2] = o
            sv = st[divmod(k, NS)]
            nc.scalar.activation(out=uo(k)[:, lo:hi, :], in_=sv[:, lo - 1 : hi - 1, :], func=ACT.Copy, scale=wgt(k, 0))

        def vprod_rest(k):
            if k // 2 not in os_:
                o = outp.tile([P, 2, SS, CS], F32, name="o")
                os_[k // 2] = o
            sv = st[divmod(k, NS)]
            nc.vector.tensor_scalar(out=uo(k)[:, 1:SS, :], in0=sv[:, 0 : SS - 1, :], scalar1=wgt(k, 0), scalar2=None, op0=ALU.mult)

        def prod_top(k):
            t, n = divmod(k, NS)
            nc.scalar.activation(out=uo(k)[:, 0, :], in_=pbs[t][:, n * CS : (n + 1) * CS], func=ACT.Copy, scale=wgt(k, 0))

        def top_pops(t):
            c = topp.tile([P, NS, CS], F32, name="topc")
            for n in range(NS):
                nc.scalar.activation(out=c[:, n, :], in_=st[(t, n)][:, 1, :], func=ACT.Copy, scale=wgt(NS * t + n, 1))
            topc[t] = c

        def top_pushes(t):
            a = topp.tile([P, NS, CS], F32, name="topa")
            for n in range(NS):
                nc.scalar.activation(out=a[:, n, :], in_=pbs[t][:, n * CS : (n + 1) * CS], func=ACT.Copy, scale=wgt(NS * t + n, 0))
            topa[t] = a

        def top_sum(t):
            b = xtp.tile([P, NS, CS], F32, name="xt")
            for n in range(NS):
                nc.tensor.matmul(out=b[:, n, :], lhsT=topa[t][:, n, :], rhs=ident[:], is_transpose=True, start=True, stop=False)
                nc.tensor.matmul(out=b[:, n, :], lhsT=topc[t][:, n, :], rhs=ident[:], is_transpose=True, start=False, stop=True)
            topb[t] = b

        def top_copy(t):
            x = topp.tile([P, NS, CS], F32, name="topx")
            nc.scalar.copy(out=x[:], in_=topb[t][:])
            topx[t] = x

        def top_back(t):
            b = xtp.tile([P, NS, CS], F32, name="xt")
            for n in range(NS):
                nc.tensor.transpose(out=b[:, n, :], in_=topx[t][:, n, :], identity=ident[:])
            topb[t] = b

        def top_last(t):
            for n in range(NS):
                k = NS * t + n
                nc.vector.scalar_tensor_tensor(out=uo(k)[:, 0, :], in0=st[(t, n)][:, 0, :], scalar=wgt(k, 2), in1=topb[t][:, n, :], op0=ALU.mult, op1=ALU.add)

        def qprod(k, lo, hi=SS - 1):
            if k // 2 not in qts:
                qt = late["qtp"].tile([P, 2, SS - 1, CS], F32, name="qt")
                qts[k // 2] = qt
            sv = st[divmod(k, NS)]
            nc.scalar.activation(out=qts[k // 2][:, k % 2, lo:hi, :], in_=sv[:, lo + 1 : hi + 1, :], func=ACT.Copy, scale=wgt(k, 1))

        def gprod(k, lo, hi=SS - 1):
            sv = st[divmod(k, NS)]
            nc.gpsimd.tensor_scalar(out=qts[k // 2][:, k % 2, lo:hi, :], in0=sv[:, lo + 1 : hi + 1, :], scalar1=wgt(k, 1), scalar2=0.0, op0=ALU.mult, op1=ALU.add)

        def gadd2(m, lo):
            o = os_[m]
            nc.gpsimd.tensor_tensor(out=o[:, :, lo : SS - 1, :], in0=o[:, :, lo : SS - 1, :], in1=qts[m][:, :, lo : SS - 1, :], op=ALU.add)

        def gadd(k, lo):
            o = uo(k)
            nc.gpsimd.tensor_tensor(out=o[:, lo : SS - 1, :], in0=o[:, lo : SS - 1, :], in1=qts[k // 2][:, k % 2, lo : SS - 1, :], op=ALU.add)

        def t1(k, lo, hi):
            o = uo(k)
            sv = st[divmod(k, NS)]
            nc.vector.scalar_tensor_tensor(out=o[:, lo:hi, :], in0=sv[:, lo:hi, :], scalar=wgt(k, 2), in1=o[:, lo:hi, :], op0=ALU.mult, op1=ALU.add)

        def spm(k):
            sv = st[divmod(k, NS)]
            sps[k] = []
            for a in range(2):
                sp = bpp.tile([P, NC], F32, name="sp")
                nc.tensor.matmul(out=sp[:], lhsT=identb[:], rhs=sv[:, 4 * a : 4 * a + 4, :].rearrange("p i c -> p (i c)"), start=True, stop=True)
                sps[k].append(sp)

        def t1p(k):
            o = uo(k)
            for a in range(2):
                nc.vector.scalar_tensor_tensor(out=o[:, 4 * a : 4 * a + 4, :], in0=sps[k][a][:].rearrange("p (i c) -> p i c", c=CS), scalar=wgt(k, 2), in1=o[:, 4 * a : 4 * a + 4, :], op0=ALU.mult, op1=ALU.add)

        def q1prod(k, n):
            q1 = late["q1p"].tile([P, G1MAX, CS], F32, name="q1")
            q1s[k] = q1
            sv = st[divmod(k, NS)]
            nc.scalar.activation(out=q1[:, 0:n, :], in_=sv[:, SS - n : SS, :], func=ACT.Copy, scale=wgt(k, 1))

        def gadd1(k, n):
            o = uo(k)
            nc.gpsimd.tensor_tensor(out=o[:, SS - 1 - n : SS - 1, :], in0=o[:, SS - 1 - n : SS - 1, :], in1=q1s[k][:, 0:n, :], op=ALU.add)

        def t2(k, lo, hi):
            o = uo(k)
            sv = st[divmod(k, NS)]
            nc.vector.scalar_tensor_tensor(out=o[:, lo:hi, :], in0=sv[:, lo + 1 : hi + 1, :], scalar=wgt(k, 1), in1=o[:, lo:hi, :], op0=ALU.mult, op1=ALU.add)

        def store0(m):
            nc.sync.dma_start(out=o0_v[:, m, :], in_=os_[m][:].rearrange("p b i c -> p (b i c)"))

        def group(ms):
            am = stat.tile([P, len(ms) * HR], F32, name="am")
            rc = stat.tile([P, len(ms) * HR], F32, name="rc")
            r4 = stat.tile([P, len(ms) * HR], F32, name="r4")
            for g, m in enumerate(ms):
                stats[m] = (am, rc, r4, g * HR)

        def red(m, b0=0, b1=2):
            am, off = stats[m][0], stats[m][3]
            nc.vector.tensor_reduce(out=am[:, off + b0 * SS : off + b1 * SS], in_=os_[m][:, b0:b1, :, :].rearrange("p b i c -> p (b i) c"), axis=AX.X, op=ALU.max, apply_absolute_value=True)

        def rcp(ms):
            am, rc = stats[ms[0]][0], stats[ms[0]][1]
            nc.vector.reciprocal(out=rc[:], in_=am[:])

        def mul(ms):
            rc, r4 = stats[ms[0]][1], stats[ms[0]][2]
            nc.scalar.activation(out=r4[:], in_=rc[:], func=ACT.Copy, scale=448.0)
            for m in ms:
                q = late["qp"].tile([P, HR, CS], FP8, name="q")
                qs[m] = q

        def vmul(m):
            rc, r4 = stats[m][1], stats[m][2]
            nc.vector.tensor_scalar(out=r4[:], in0=rc[:], scalar1=448.0, scalar2=None, op0=ALU.mult)
            q = late["qp"].tile([P, HR, CS], FP8, name="q")
            qs[m] = q

        def scasts(m, cv):
            r4, off = stats[m][2], stats[m][3]
            ov = os_[m][:].rearrange("p b i c -> p (b i) c")
            for j in range(cv, HR):
                nc.scalar.activation(out=qs[m][:, j, :], in_=ov[:, j, :], func=ACT.Identity, scale=r4[:, off + j : off + j + 1], bias=zero[:, 0:1], saturate=False)

        def vcasts(m, cv, c0=0):
            r4, off = stats[m][2], stats[m][3]
            ov = os_[m][:].rearrange("p b i c -> p (b i) c")
            for j in range(c0, cv):
                nc.vector.tensor_scalar(out=qs[m][:, j, :], in0=ov[:, j, :], scalar1=r4[:, off + j : off + j + 1], scalar2=None, op0=ALU.mult, saturate=False)

        def store1(m, j0=0, j1=HR):
            nc.sync.dma_start(out=o1_v[:, m, j0 * CS : j1 * CS], in_=qs[m][:, j0:j1, :].bitcast(U8).rearrange("p j c -> p (j c)"))

        def tops(ks):
            for k in ks:
                prod_top(k)
            for k in ks:
                t1(k, 0, 1)
            for k in ks:
                t2(k, 0, 1)

        ctx.enter_context(tc.manual_schedule(engines={ENG.DVE, ENG.Pool, ENG.Activation, ENG.PE}))

        nc.sync.dma_start(out=lg[:], in_=lg_v)
        for n in range(NS):
            s0 = const.tile([P, UNIT], BF16, name="st0_%d" % n)
            nc.sync.dma_start(out=s0[:], in_=st_v[:, 0, n, :])
            st[(0, n)] = s0[:].rearrange("p (i c) -> p i c", c=CS)
        nc.gpsimd.memset(brow[:], 0.0)
        nc.sync.dma_start(out=brow[0:1, :], in_=b_push.rearrange("(o n) -> o n", o=1))

        def load_stacks(t):
            s1 = const.tile([P, NS, UNIT], BF16, name="st%d" % t)
            nc.sync.dma_start(out=s1[:], in_=st_v[:, t, :, :])
            for n in range(NS):
                st[(t, n)] = s1[:, n, :].rearrange("p (i c) -> p i c", c=CS)

        load_stacks(1)
        with tc.tile_pool(name="wtmp", bufs=1) as wtmp:
            wraw = []
            for j in range(NS):
                wr = wtmp.tile([P, H], BF16, name="wraw%d" % j)
                nc.sync.dma_start(out=wr[:], in_=w_v[:, j, :])
                wraw.append(wr)
            for t in range(NT):
                hr = const.tile([P, H], BF16, name="hraw%d" % t)
                nc.sync.dma_start(out=hr[:], in_=h_v[:, t, :])
                hraw.append(hr)
                if t >= 2:
                    load_stacks(t)

            nc.vector.memset(zero[:], 0.0)
            nc.scalar.activation(out=warm[:], in_=zero[:], func=ACT.Exp)
            make_identity(nc, ident[:])
            nc.gpsimd.memset(ones[:], 1.0)
            make_identity(nc, identb[:])

            lg3 = lg[:].rearrange("p (t l) -> p t l", l=L)
            mx_ = const.tile([P, NT], F32, name="mx_")
            nc.vector.tensor_reduce(out=mx_[:], in_=lg3, axis=AX.X, op=ALU.max)
            dd = const.tile([P, NT, L], F32, name="dd")
            nc.vector.tensor_tensor(out=dd[:], in0=lg3, in1=mx_[:].unsqueeze(2).to_broadcast([P, NT, L]), op=ALU.subtract)
            ee = const.tile([P, NT, L], F32, name="ee")
            nc.scalar.activation(out=ee[:], in_=dd[:], func=ACT.Exp)
            sm = const.tile([P, NT], F32, name="sm")
            nc.vector.tensor_reduce(out=sm[:], in_=ee[:], axis=AX.X, op=ALU.add)
            rs = const.tile([P, NT], F32, name="rs")
            nc.vector.reciprocal(out=rs[:], in_=sm[:])
            nc.vector.tensor_tensor(out=act[:], in0=ee[:], in1=rs[:].unsqueeze(2).to_broadcast([P, NT, L]), op=ALU.mult)

            wgs = []
            for g in range(NPASS):
                wg = wtmp.tile([P, NC * PACK], BF16, name="wg%d" % g, align_bytes=64)
                wgs.append(wg)

            def w_turn(g, jj):
                wgw = wgs[g][:].bitcast(F32).rearrange("p (j r u) -> p j r u", j=NS, u=2)
                xt = xtp.tile([P, 2, 2, P], F32, name="xt")
                for a in range(2):
                    words = wraw[jj + a][:].bitcast(F32)
                    for u in range(2):
                        nc.tensor.transpose(out=xt[:, a, u, :], in_=words[:, 256 * g + u : 256 * (g + 1) : 2], identity=ident[:])
                nc.scalar.copy(out=wgw[:, jj : jj + 2, :, :], in_=xt[:].rearrange("p a u r -> p a r u"))

            def w_quant(g):
                nc.vector.quantize_mx(out=wc[:, g * NC : (g + 1) * NC].bitcast(FP8X4), scales=ws[:, g * NC : (g + 1) * NC], in_=wgs[g][:])

            prod_rest(0, 1, 4)
            prod_rest(0, 4, SS)
            for k in range(1, 6):
                prod_rest(k)
            top_pops(0)
            bps = bpp.tile([P, NC], F32, name="sp")
            nc.tensor.matmul(out=bps[:], lhsT=ones[:], rhs=brow[:], start=True, stop=True)
            nc.scalar.copy(out=bias[:], in_=bps[:])
            for jj in (0, 2):
                for g in range(NPASS):
                    w_turn(g, jj)
            h_turn(0)
            h_copy(0)
            t1(0, 1, 4)
            t1(0, 4, SS)
            t1(1, 1, SS)
            for k in range(2, 4):
                t2(k - 2, 1, SS - 1)
                t1(k, 1, SS)
            t2(2, 1, SS - 1)
            t2(3, 1, SS - 1)
            vprod_rest(6)
            t1(4, 1, SS)
            for g in range(NPASS):
                w_quant(g)
            t1(5, 1, SS)
            h_quant(0)

        late["qtp"] = ctx.enter_context(tc.tile_pool(name="qtp", bufs=3))
        late["qp"] = ctx.enter_context(tc.tile_pool(name="qp", bufs=4))
        late["q1p"] = ctx.enter_context(tc.tile_pool(name="q1p", bufs=1))

        h_turn(1)
        h_copy(1)
        t1(6, 1, SS)
        t2(4, 1, SS - 1)
        h_quant(1)
        mm(0)
        prod_rest(8)
        t1(8, 1, SS)
        h_turn(2)
        prod_rest(10)
        badd(0)
        h_copy(2)
        top_pushes(0)
        h_turn(3)
        top_sum(0)
        h_copy(3)
        top_copy(0)
        vprod_rest(7)
        t1(10, 1, SS)
        h_quant(2)
        mm(1)
        top_back(0)
        h_quant(3)
        mm(2)
        for k in (6, 7, 5):
            qprod(k, 1)
        t1(7, 1, SS)
        prod_rest(11)
        prod_rest(9)
        qprod(9, 0)
        qprod(8, 0)

        cast_q = [0, 1]
        red_q = [2, 3]
        gadd2(3, 1)
        gadd(5, 1)
        top_last(0)
        store0(0)
        store0(1)
        group([0, 1])
        red(0)
        badd(1)
        mm(3)
        h_turn(4)
        red(1)
        badd(2)
        badd(3)
        rcp([0, 1])
        tops([4, 5, 6, 7])
        store0(2)
        store0(3)
        for k in (8, 10, 11, 9):
            prod_top(k)
        h_copy(4)
        qprod(10, 0)
        qprod(11, 0)

        for t in range(2, NT):
            last = t == NT - 1
            todo = list(cast_q)
            cast_q.clear()
            mul(todo)
            if not last:
                for k in range(NS * (t + 1), NS * (t + 2)):
                    prod_rest(k)
                    prod_top(k)
                    if k % NS == 1 and t + 3 < NT:
                        h_trans(t + 3)
                qprod(NS * (t + 1) + 2, 0)
                if GP[t] < SS - 1:
                    qprod(NS * (t + 1) + 3, 0, SS - 1 - GP[t])
                spm(NS * (t + 1))
            if 2 < t < NT - 2:
                mm(t + 2)
            for m in todo:
                scasts(m, CV_STEADY)
            k0 = NS * t
            if t == 2:
                t1(k0, 0, 1)
                t1(k0 + 2, 0, 1)
                t1(k0 + 3, 0, SS)
                h_quant(4)
                mm(4)
                t1(k0 + 1, 0, SS)
                gadd2(2 * t, 0)
                store0(2 * t)
            else:
                t2(k0, 0, SS - 1)
                t2(k0 + 1, 0, SS - 1 - G1[t])
                t1(k0 + 2, 0, SS)
                t1(k0 + 3, 0, SS)
                t1(k0 + 1, 0, SS)
                if G1[t]:
                    gadd1(k0 + 1, G1[t])
                store0(2 * t)
            gadd2(2 * t + 1, 0)
            store0(2 * t + 1)
            if GP[t]:
                gprod(NS * (t + 1) + 3, SS - 1 - GP[t])
            reds = red_q + [2 * t]
            red_q = [2 * t + 1]
            if last:
                for m in reds:
                    group([m])
                    red(m)
                    rcp([m])
            else:
                group(reds)
                for m in reds:
                    red(m)
                if t + 2 < NT:
                    badd(t + 2)
                rcp(reds)
            cast_q.extend(reds)
            if not last:
                t1p(NS * (t + 1))
            if t + 3 < NT:
                h_quant(t + 3)
            if not last and G1[t + 1]:
                q1prod(NS * (t + 1) + 1, G1[t + 1])
            for m in todo:
                vcasts(m, CV_STEADY)
                store1(m)

        mlast = NH - 1
        group([mlast])
        red(mlast, 0, 1)
        red(mlast, 1, 2)
        for m in cast_q:
            mul([m])
            scasts(m, CV_TAIL[m])
        for m in cast_q:
            vcasts(m, CV_TAIL[m])
            store1(m)
        rcp([mlast])
        vmul(mlast)
        scasts(mlast, CV_LAST)
        vcasts(mlast, SS)
        store1(mlast, 0, SS)
        vcasts(mlast, CV_LAST, SS)
        store1(mlast, SS, HR)
